import numpy as np
import ml_dtypes


def mxq(x, axis, fmt="e4m3"):
    dtype, down = {"e4m3": (ml_dtypes.float8_e4m3fn, 7), "e5m2": (ml_dtypes.float8_e5m2, 14)}[fmt]
    v = np.moveaxis(np.asarray(x, np.float32).astype(ml_dtypes.bfloat16).astype(np.float64), axis, -1)
    blocks = v.reshape(v.shape[:-1] + (-1, 32))
    amax = np.abs(blocks).max(-1, keepdims=True)
    byte = np.maximum(np.where(amax > 0, np.frexp(amax)[1] - 1 + 127, 0) - down, 1)
    scale = np.exp2(byte - 127.0)
    codes = (blocks / scale).astype(np.float32).astype(dtype).astype(np.float64)
    return np.moveaxis((codes * scale).reshape(v.shape), -1, axis)


WIDE = False


def mx_kscale(k):
    if not WIDE:
        return np.ones(k)
    levels = np.array([20, -20, 10, -10, 0])
    a = np.random.permutation(np.resize(levels, k // 512 * 4)).reshape(k // 512, 4)
    idx = np.arange(k)
    return np.exp2(a[idx // 512, idx % 128 // 32])


BF16 = ml_dtypes.bfloat16


def bf(x):
    return np.asarray(x, np.float32).astype(BF16)


def f64(x):
    return np.asarray(x).astype(np.float64)


B, L, H = 2, 1024, 1024
HH = H // 2
BASE = 10000.0


def rope_tables():
    inv_freq = 1.0 / BASE ** (np.arange(0, H, 2) / H)
    freqs = np.outer(np.arange(L), inv_freq)
    emb = np.concatenate([freqs, freqs], axis=-1)
    return np.cos(emb), np.sin(emb)


def rotate_half(x):
    x1, x2 = np.split(x, 2, axis=-1)
    return np.concatenate([-x2, x1], axis=-1)


def rotate_half_t(y):
    y1, y2 = np.split(y, 2, axis=-1)
    return np.concatenate([y2, -y1], axis=-1)


def setup_inputs():
    u = mx_kscale(H)
    cos, sin = rope_tables()
    x = np.random.standard_normal((B, L, H)) * 0.2
    w = np.random.standard_normal((H, H)) * 0.5 / np.sqrt(H) / u[:, None]
    g = np.random.standard_normal((B, L, H)) * np.exp2(np.random.randint(-12, 1, (B, L, 1))) * 16.0 * u
    return {"hidden_states": bf(x), "W_q": bf(w), "cos": bf(cos), "sin": bf(sin), "grad_out": bf(g)}


def reference(hidden_states, W_q, cos, sin, grad_out):
    gh = mxq(f64(grad_out), 2, "e5m2") @ mxq(f64(W_q), 0, "e4m3")
    return gh * f64(cos)[None, :, :] + rotate_half_t(gh * f64(sin)[None, :, :])

@@ -1,0 +1,136 @@
+import concourse.mybir as mybir
+from concourse.masks import make_identity
+
+F32 = mybir.dt.float32
+BF16 = mybir.dt.bfloat16
+U32 = mybir.dt.uint32
+U8 = mybir.dt.uint8
+E4M3_X4 = mybir.dt.float8_e4m3fn_x4
+E5M2_X4 = mybir.dt.float8_e5m2_x4
+MULT = mybir.AluOpType.mult
+ADD = mybir.AluOpType.add
+
+BATCH, LENGTH, WIDTH = 2, 1024, 1024
+HALF = WIDTH // 2
+P = 128
+PACK = 4
+K_PASS = P * PACK
+PASSES = WIDTH // K_PASS
+L_BLOCKS = LENGTH // P
+PAIR = 2
+RUN = 4
+AHEAD = 2
+
+FLOPS = 2 * BATCH * LENGTH * WIDTH * WIDTH
+BYTES = 2 * (BATCH * LENGTH * WIDTH + 3 * WIDTH * WIDTH) + 4 * BATCH * LENGTH * WIDTH
+
+
+def tile_denseattentiononehead_pa_kernel(tc, hidden_states, W_q, cos, sin, grad_out, out):
+    nc = tc.nc
+    with (
+        tc.tile_pool(name="resident", bufs=1) as resident,
+        tc.tile_pool(name="w_stage", bufs=PASSES * 2) as w_stage,
+        tc.tile_pool(name="g_stage", bufs=AHEAD + 2) as g_stage,
+        tc.tile_pool(name="products", bufs=3) as products,
+        tc.tile_pool(name="results", bufs=6) as results,
+        tc.psum_pool(name="transposed", bufs=2) as transposed,
+        tc.psum_pool(name="gh", bufs=3) as gh_pool,
+    ):
+        g_rows = []
+        cos_rows = []
+        sin_rows = []
+        w_rows = []
+        for n in range(L_BLOCKS):
+            positions = slice(n * P, (n + 1) * P)
+            g_tile = resident.tile([P, BATCH * WIDTH], BF16, name="g_rows%d" % n)
+            nc.sync.dma_start(
+                out=g_tile[:].rearrange("p (b o) -> p b o", b=BATCH),
+                in_=grad_out[:, positions, :].rearrange("b p o -> p b o"),
+            )
+            g_rows.append(g_tile)
+            if n == 0:
+                for c in range(PASSES):
+                    w_tile = resident.tile([P, PACK, WIDTH], BF16, name="w_rows%d" % c)
+                    nc.sync.dma_start(
+                        out=w_tile[:],
+                        in_=W_q[c * K_PASS : (c + 1) * K_PASS, :].rearrange("(p t) j -> p t j", t=PACK),
+                    )
+                    w_rows.append(w_tile)
+            cos_tile = resident.tile([P, WIDTH], BF16, name="cos_rows%d" % n)
+            nc.sync.dma_start(out=cos_tile[:], in_=cos[positions, :])
+            cos_rows.append(cos_tile)
+            sin_tile = resident.tile([P, WIDTH], BF16, name="sin_rows%d" % n)
+            nc.sync.dma_start(out=sin_tile[:], in_=sin[positions, :])
+            sin_rows.append(sin_tile)
+
+        identity = resident.tile([P, P], F32, name="identity")
+        make_identity(nc, identity[:])
+
+        def transpose_and_quantise_tokens(n, b):
+            words = g_rows[n][:].bitcast(F32).rearrange(
+                "p (b c q u) -> p b c q u", b=BATCH, c=PASSES, u=PAIR
+            )
+            turned = transposed.tile([P, PASSES, PAIR, P], F32)
+            for c in range(PASSES):
+                for u in range(PAIR):
+                    nc.tensor.transpose(turned[:, c, u, :], words[:, b, c, :, u], identity[:])
+            g_grouped = g_stage.tile([P, PASSES * P * PACK], BF16, align_bytes=64)
+            nc.scalar.copy(
+                out=g_grouped[:].bitcast(F32).rearrange("p (c r u) -> p c r u", c=PASSES, u=PAIR),
+                in_=turned[:].rearrange("p c u r -> p c r u"),
+            )
+            g_codes = g_stage.tile([P, PASSES * P], U32, align_bytes=64)
+            g_scales = g_stage.tile([P, PASSES * P], U8, align_bytes=64)
+            nc.vector.quantize_mx(out=g_codes[:].bitcast(E5M2_X4), scales=g_scales[:], in_=g_grouped[:])
+            return g_codes, g_scales
+
+        tiles = [(n, b) for n in range(L_BLOCKS) for b in range(BATCH)]
+        quantised = [transpose_and_quantise_tokens(n, b) for (n, b) in tiles[:AHEAD]]
+
+        w_codes = resident.tile([P, PASSES, WIDTH], U32, name="w_codes", align_bytes=64)
+        w_scales = resident.tile([P, PASSES, WIDTH], U8, name="w_scales", align_bytes=64)
+        for c in range(PASSES):
+            for h in range(2):
+                columns = slice(h * HALF, (h + 1) * HALF)
+                w_grouped = w_stage.tile([P, HALF * PACK], BF16, align_bytes=64)
+                regroup = nc.vector.tensor_copy if h == 0 else nc.scalar.copy
+                regroup(
+                    out=w_grouped[:].rearrange("p (m i t) -> p m t i", i=RUN, t=PACK),
+                    in_=w_rows[c][:, :, columns].rearrange("p t (m i) -> p m t i", i=RUN),
+                )
+                nc.vector.quantize_mx(
+                    out=w_codes[:, c, columns].bitcast(E4M3_X4),
+                    scales=w_scales[:, c, columns],
+                    in_=w_grouped[:],
+                )
+
+        for i, (n, b) in enumerate(tiles):
+            if i + AHEAD < len(tiles):
+                quantised.append(transpose_and_quantise_tokens(*tiles[i + AHEAD]))
+            g_codes, g_scales = quantised[i]
+
+            gh_low = gh_pool.tile([P, HALF], F32)
+            gh_high = gh_pool.tile([P, HALF], F32)
+            for h, gh_half in enumerate((gh_low, gh_high)):
+                for c in range(PASSES):
+                    nc.tensor.matmul_mx(
+                        out=gh_half[:],
+                        lhsT=g_codes[:, c * P : (c + 1) * P].bitcast(E5M2_X4),
+                        lhsT_scale=g_scales[:, c * P : (c + 1) * P],
+                        rhs=w_codes[:, c, h * HALF : (h + 1) * HALF].bitcast(E4M3_X4),
+                        rhs_scale=w_scales[:, c, h * HALF : (h + 1) * HALF],
+                        start=(c == 0),
+                        stop=(c == PASSES - 1),
+                    )
+
+            low, high = slice(0, HALF), slice(HALF, WIDTH)
+            by_cos = results.tile([P, WIDTH], F32)
+            by_sin = products.tile([P, WIDTH], F32)
+            nc.vector.tensor_tensor(out=by_cos[:, low], in0=gh_low[:], in1=cos_rows[n][:, low], op=MULT)
+            nc.vector.scalar_tensor_tensor(
+                out=by_sin[:, high], in0=gh_low[:], scalar=-1.0, in1=sin_rows[n][:, low], op0=MULT, op1=MULT
+            )
+            nc.vector.tensor_tensor(out=by_cos[:, high], in0=gh_high[:], in1=cos_rows[n][:, high], op=MULT)
+            nc.vector.tensor_tensor(out=by_sin[:, low], in0=gh_high[:], in1=sin_rows[n][:, high], op=MULT)
+            nc.gpsimd.tensor_tensor(out=by_cos[:], in0=by_cos[:], in1=by_sin[:], op=ADD)
+            nc.sync.dma_start(out=out[b, n * P : (n + 1) * P, :], in_=by_cos[:])

@@ -19,7 +19,6 @@ PASSES = WIDTH // K_PASS
 L_BLOCKS = LENGTH // P
 PAIR = 2
 RUN = 4
-AHEAD = 2
 
 FLOPS = 2 * BATCH * LENGTH * WIDTH * WIDTH
 BYTES = 2 * (BATCH * LENGTH * WIDTH + 3 * WIDTH * WIDTH) + 4 * BATCH * LENGTH * WIDTH
@@ -27,110 +26,142 @@ BYTES = 2 * (BATCH * LENGTH * WIDTH + 3 * WIDTH * WIDTH) + 4 * BATCH * LENGTH * 
 
 def tile_denseattentiononehead_pa_kernel(tc, hidden_states, W_q, cos, sin, grad_out, out):
     nc = tc.nc
+    low, high = slice(0, HALF), slice(HALF, WIDTH)
+    halves = (low, high)
     with (
         tc.tile_pool(name="resident", bufs=1) as resident,
         tc.tile_pool(name="w_stage", bufs=PASSES * 2) as w_stage,
-        tc.tile_pool(name="g_stage", bufs=AHEAD + 2) as g_stage,
-        tc.tile_pool(name="products", bufs=3) as products,
-        tc.tile_pool(name="results", bufs=6) as results,
+        tc.tile_pool(name="g_stage", bufs=3) as g_stage,
+        tc.tile_pool(name="products", bufs=3 * BATCH) as products,
+        tc.tile_pool(name="results", bufs=5 * BATCH) as results,
         tc.psum_pool(name="transposed", bufs=2) as transposed,
         tc.psum_pool(name="gh", bufs=3) as gh_pool,
+        tc.manual_schedule(),
     ):
-        g_rows = []
-        cos_rows = []
-        sin_rows = []
-        w_rows = []
-        for n in range(L_BLOCKS):
+        def load_w(h, c):
+            w_tile = resident.tile([P, PACK, HALF], BF16, name="w_rows%d%d" % (h, c))
+            nc.sync.dma_start(
+                out=w_tile[:],
+                in_=W_q[c * K_PASS : (c + 1) * K_PASS, halves[h]].rearrange("(p t) j -> p t j", t=PACK),
+            )
+            return w_tile
+
+        def load_block(n):
             positions = slice(n * P, (n + 1) * P)
             g_tile = resident.tile([P, BATCH * WIDTH], BF16, name="g_rows%d" % n)
             nc.sync.dma_start(
                 out=g_tile[:].rearrange("p (b o) -> p b o", b=BATCH),
                 in_=grad_out[:, positions, :].rearrange("b p o -> p b o"),
             )
-            g_rows.append(g_tile)
-            if n == 0:
-                for c in range(PASSES):
-                    w_tile = resident.tile([P, PACK, WIDTH], BF16, name="w_rows%d" % c)
-                    nc.sync.dma_start(
-                        out=w_tile[:],
-                        in_=W_q[c * K_PASS : (c + 1) * K_PASS, :].rearrange("(p t) j -> p t j", t=PACK),
-                    )
-                    w_rows.append(w_tile)
             cos_tile = resident.tile([P, WIDTH], BF16, name="cos_rows%d" % n)
             nc.sync.dma_start(out=cos_tile[:], in_=cos[positions, :])
-            cos_rows.append(cos_tile)
             sin_tile = resident.tile([P, WIDTH], BF16, name="sin_rows%d" % n)
             nc.sync.dma_start(out=sin_tile[:], in_=sin[positions, :])
-            sin_rows.append(sin_tile)
+            return g_tile, cos_tile, sin_tile
+
+        w_rows = {}
+        for c in range(PASSES):
+            w_rows[(0, c)] = load_w(0, c)
+        blocks = [load_block(0)]
+        for c in range(PASSES):
+            w_rows[(1, c)] = load_w(1, c)
+        for n in range(1, L_BLOCKS):
+            blocks.append(load_block(n))
 
         identity = resident.tile([P, P], F32, name="identity")
         make_identity(nc, identity[:])
 
-        def transpose_and_quantise_tokens(n, b):
-            words = g_rows[n][:].bitcast(F32).rearrange(
+        w_codes = resident.tile([P, PASSES, WIDTH], U32, name="w_codes", align_bytes=64)
+        w_scales = resident.tile([P, PASSES, WIDTH], U8, name="w_scales", align_bytes=64)
+
+        def quantise_w(h, c, regroup):
+            w_grouped = w_stage.tile([P, HALF * PACK], BF16, align_bytes=64)
+            regroup(
+                out=w_grouped[:].rearrange("p (m i t) -> p m t i", i=RUN, t=PACK),
+                in_=w_rows[(h, c)][:].rearrange("p t (m i) -> p m t i", i=RUN),
+            )
+            nc.vector.quantize_mx(
+                out=w_codes[:, c, halves[h]].bitcast(E4M3_X4),
+                scales=w_scales[:, c, halves[h]],
+                in_=w_grouped[:],
+            )
+
+        def quantise_tokens(n):
+            words = blocks[n][0][:].bitcast(F32).rearrange(
                 "p (b c q u) -> p b c q u", b=BATCH, c=PASSES, u=PAIR
             )
-            turned = transposed.tile([P, PASSES, PAIR, P], F32)
-            for c in range(PASSES):
-                for u in range(PAIR):
-                    nc.tensor.transpose(turned[:, c, u, :], words[:, b, c, :, u], identity[:])
-            g_grouped = g_stage.tile([P, PASSES * P * PACK], BF16, align_bytes=64)
-            nc.scalar.copy(
-                out=g_grouped[:].bitcast(F32).rearrange("p (c r u) -> p c r u", c=PASSES, u=PAIR),
-                in_=turned[:].rearrange("p c u r -> p c r u"),
+            g_grouped = g_stage.tile([P, BATCH * PASSES * P * PACK], BF16, align_bytes=64)
+            grouped_words = g_grouped[:].bitcast(F32).rearrange(
+                "p (b c r u) -> p b c r u", b=BATCH, c=PASSES, u=PAIR
             )
-            g_codes = g_stage.tile([P, PASSES * P], U32, align_bytes=64)
-            g_scales = g_stage.tile([P, PASSES * P], U8, align_bytes=64)
+            for b in range(BATCH):
+                turned = transposed.tile([P, PASSES, PAIR, P], F32)
+                for c in range(PASSES):
+                    for u in range(PAIR):
+                        nc.tensor.transpose(turned[:, c, u, :], words[:, b, c, :, u], identity[:])
+                nc.scalar.copy(out=grouped_words[:, b], in_=turned[:].rearrange("p c u r -> p c r u"))
+            g_codes = g_stage.tile([P, BATCH * PASSES * P], U32, align_bytes=64)
+            g_scales = g_stage.tile([P, BATCH * PASSES * P], U8, align_bytes=64)
             nc.vector.quantize_mx(out=g_codes[:].bitcast(E5M2_X4), scales=g_scales[:], in_=g_grouped[:])
             return g_codes, g_scales
 
-        tiles = [(n, b) for n in range(L_BLOCKS) for b in range(BATCH)]
-        quantised = [transpose_and_quantise_tokens(n, b) for (n, b) in tiles[:AHEAD]]
-
-        w_codes = resident.tile([P, PASSES, WIDTH], U32, name="w_codes", align_bytes=64)
-        w_scales = resident.tile([P, PASSES, WIDTH], U8, name="w_scales", align_bytes=64)
-        for c in range(PASSES):
-            for h in range(2):
-                columns = slice(h * HALF, (h + 1) * HALF)
-                w_grouped = w_stage.tile([P, HALF * PACK], BF16, align_bytes=64)
-                regroup = nc.vector.tensor_copy if h == 0 else nc.scalar.copy
-                regroup(
-                    out=w_grouped[:].rearrange("p (m i t) -> p m t i", i=RUN, t=PACK),
-                    in_=w_rows[c][:, :, columns].rearrange("p t (m i) -> p m t i", i=RUN),
+        def multiply(tokens, b, h):
+            g_codes, g_scales = tokens
+            gh_half = gh_pool.tile([P, HALF], F32, tag="gh_half%d" % h)
+            for c in range(PASSES):
+                token_columns = slice((b * PASSES + c) * P, (b * PASSES + c + 1) * P)
+                nc.tensor.matmul_mx(
+                    out=gh_half[:],
+                    lhsT=g_codes[:, token_columns].bitcast(E5M2_X4),
+                    lhsT_scale=g_scales[:, token_columns],
+                    rhs=w_codes[:, c, halves[h]].bitcast(E4M3_X4),
+                    rhs_scale=w_scales[:, c, halves[h]],
+                    start=(c == 0),
+                    stop=(c == PASSES - 1),
                 )
-                nc.vector.quantize_mx(
-                    out=w_codes[:, c, columns].bitcast(E4M3_X4),
-                    scales=w_scales[:, c, columns],
-                    in_=w_grouped[:],
+            return gh_half
+
+        def low_stage(n, tokens):
+            cos_rows, sin_rows = blocks[n][1], blocks[n][2]
+            gh_low = [multiply(tokens, b, 0) for b in range(BATCH)]
+            by_cos = []
+            by_sin = []
+            for b in range(BATCH):
+                by_cos.append(results.tile([P, WIDTH], F32, name="by_cos", tag="by_cos"))
+                by_sin.append(products.tile([P, WIDTH], F32, name="by_sin", tag="by_sin"))
+                nc.vector.tensor_tensor(out=by_cos[b][:, low], in0=gh_low[b][:], in1=cos_rows[:, low], op=MULT)
+                nc.vector.scalar_tensor_tensor(
+                    out=by_sin[b][:, high], in0=gh_low[b][:], scalar=-1.0, in1=sin_rows[:, low], op0=MULT, op1=MULT
                 )
+            return by_cos, by_sin
 
-        for i, (n, b) in enumerate(tiles):
-            if i + AHEAD < len(tiles):
-                quantised.append(transpose_and_quantise_tokens(*tiles[i + AHEAD]))
-            g_codes, g_scales = quantised[i]
+        def high_stage(n, tokens, by_cos, by_sin):
+            cos_rows, sin_rows = blocks[n][1], blocks[n][2]
+            gh_high = [multiply(tokens, b, 1) for b in range(BATCH)]
+            for b in range(BATCH):
+                rows = out[b, n * P : (n + 1) * P, :]
+                nc.vector.tensor_tensor(out=by_sin[b][:, low], in0=gh_high[b][:], in1=sin_rows[:, high], op=MULT)
+                nc.vector.tensor_tensor(out=by_cos[b][:, high], in0=gh_high[b][:], in1=cos_rows[:, high], op=MULT)
+                if (n, b) != (L_BLOCKS - 1, BATCH - 1):
+                    nc.gpsimd.tensor_tensor(out=by_cos[b][:], in0=by_cos[b][:], in1=by_sin[b][:], op=ADD)
+                    nc.sync.dma_start(out=rows, in_=by_cos[b][:])
+                else:
+                    for half in halves:
+                        nc.vector.tensor_tensor(
+                            out=by_cos[b][:, half], in0=by_cos[b][:, half], in1=by_sin[b][:, half], op=ADD
+                        )
+                        nc.sync.dma_start(out=rows[:, half], in_=by_cos[b][:, half])
 
-            gh_low = gh_pool.tile([P, HALF], F32)
-            gh_high = gh_pool.tile([P, HALF], F32)
-            for h, gh_half in enumerate((gh_low, gh_high)):
-                for c in range(PASSES):
-                    nc.tensor.matmul_mx(
-                        out=gh_half[:],
-                        lhsT=g_codes[:, c * P : (c + 1) * P].bitcast(E5M2_X4),
-                        lhsT_scale=g_scales[:, c * P : (c + 1) * P],
-                        rhs=w_codes[:, c, h * HALF : (h + 1) * HALF].bitcast(E4M3_X4),
-                        rhs_scale=w_scales[:, c, h * HALF : (h + 1) * HALF],
-                        start=(c == 0),
-                        stop=(c == PASSES - 1),
-                    )
-
-            low, high = slice(0, HALF), slice(HALF, WIDTH)
-            by_cos = results.tile([P, WIDTH], F32)
-            by_sin = products.tile([P, WIDTH], F32)
-            nc.vector.tensor_tensor(out=by_cos[:, low], in0=gh_low[:], in1=cos_rows[n][:, low], op=MULT)
-            nc.vector.scalar_tensor_tensor(
-                out=by_sin[:, high], in0=gh_low[:], scalar=-1.0, in1=sin_rows[n][:, low], op0=MULT, op1=MULT
-            )
-            nc.vector.tensor_tensor(out=by_cos[:, high], in0=gh_high[:], in1=cos_rows[n][:, high], op=MULT)
-            nc.vector.tensor_tensor(out=by_sin[:, low], in0=gh_high[:], in1=sin_rows[n][:, high], op=MULT)
-            nc.gpsimd.tensor_tensor(out=by_cos[:], in0=by_cos[:], in1=by_sin[:], op=ADD)
-            nc.sync.dma_start(out=out[b, n * P : (n + 1) * P, :], in_=by_cos[:])
+        quantise_w(0, 0, nc.vector.tensor_copy)
+        quantise_w(0, 1, nc.vector.tensor_copy)
+        tokens = quantise_tokens(0)
+        sums = low_stage(0, tokens)
+        quantise_w(1, 0, nc.scalar.copy)
+        quantise_w(1, 1, nc.vector.tensor_copy)
+        for n in range(L_BLOCKS):
+            if n + 1 < L_BLOCKS:
+                next_tokens = quantise_tokens(n + 1)
+            high_stage(n, tokens, *sums)
+            if n + 1 < L_BLOCKS:
+                tokens = next_tokens
+                sums = low_stage(n + 1, tokens)

@@ -19,6 +19,7 @@ PASSES = WIDTH // K_PASS
 L_BLOCKS = LENGTH // P
 PAIR = 2
 RUN = 4
+AHEAD = 2
 
 FLOPS = 2 * BATCH * LENGTH * WIDTH * WIDTH
 BYTES = 2 * (BATCH * LENGTH * WIDTH + 3 * WIDTH * WIDTH) + 4 * BATCH * LENGTH * WIDTH
@@ -31,7 +32,7 @@ def tile_denseattentiononehead_pa_kernel(tc, hidden_states, W_q, cos, sin, grad_
     with (
         tc.tile_pool(name="resident", bufs=1) as resident,
         tc.tile_pool(name="w_stage", bufs=PASSES * 2) as w_stage,
-        tc.tile_pool(name="g_stage", bufs=3) as g_stage,
+        tc.tile_pool(name="g_stage", bufs=AHEAD + 2) as g_stage,
         tc.tile_pool(name="products", bufs=3 * BATCH) as products,
         tc.tile_pool(name="results", bufs=5 * BATCH) as results,
         tc.psum_pool(name="transposed", bufs=2) as transposed,
@@ -46,27 +47,34 @@ def tile_denseattentiononehead_pa_kernel(tc, hidden_states, W_q, cos, sin, grad_
             )
             return w_tile
 
-        def load_block(n):
-            positions = slice(n * P, (n + 1) * P)
+        def load_tokens(n):
             g_tile = resident.tile([P, BATCH * WIDTH], BF16, name="g_rows%d" % n)
             nc.sync.dma_start(
                 out=g_tile[:].rearrange("p (b o) -> p b o", b=BATCH),
-                in_=grad_out[:, positions, :].rearrange("b p o -> p b o"),
+                in_=grad_out[:, n * P : (n + 1) * P, :].rearrange("b p o -> p b o"),
             )
-            cos_tile = resident.tile([P, WIDTH], BF16, name="cos_rows%d" % n)
-            nc.sync.dma_start(out=cos_tile[:], in_=cos[positions, :])
-            sin_tile = resident.tile([P, WIDTH], BF16, name="sin_rows%d" % n)
-            nc.sync.dma_start(out=sin_tile[:], in_=sin[positions, :])
-            return g_tile, cos_tile, sin_tile
+            return g_tile
 
+        def load_tables(n):
+            cos_tile = resident.tile([P, WIDTH], BF16, name="cos_rows%d" % n)
+            nc.sync.dma_start(out=cos_tile[:], in_=cos[n * P : (n + 1) * P, :])
+            sin_tile = resident.tile([P, WIDTH], BF16, name="sin_rows%d" % n)
+            nc.sync.dma_start(out=sin_tile[:], in_=sin[n * P : (n + 1) * P, :])
+            return cos_tile, sin_tile
+
+        g_rows = [load_tokens(0)]
         w_rows = {}
         for c in range(PASSES):
             w_rows[(0, c)] = load_w(0, c)
-        blocks = [load_block(0)]
+        tables = [load_tables(0)]
         for c in range(PASSES):
             w_rows[(1, c)] = load_w(1, c)
+        for n in range(1, AHEAD):
+            g_rows.append(load_tokens(n))
         for n in range(1, L_BLOCKS):
-            blocks.append(load_block(n))
+            if n + AHEAD - 1 < L_BLOCKS:
+                g_rows.append(load_tokens(n + AHEAD - 1))
+            tables.append(load_tables(n))
 
         identity = resident.tile([P, P], F32, name="identity")
         make_identity(nc, identity[:])
@@ -86,10 +94,8 @@ def tile_denseattentiononehead_pa_kernel(tc, hidden_states, W_q, cos, sin, grad_
                 in_=w_grouped[:],
             )
 
-        def quantise_tokens(n):
-            words = blocks[n][0][:].bitcast(F32).rearrange(
-                "p (b c q u) -> p b c q u", b=BATCH, c=PASSES, u=PAIR
-            )
+        def turn_tokens(n):
+            words = g_rows[n][:].bitcast(F32).rearrange("p (b c q u) -> p b c q u", b=BATCH, c=PASSES, u=PAIR)
             g_grouped = g_stage.tile([P, BATCH * PASSES * P * PACK], BF16, align_bytes=64)
             grouped_words = g_grouped[:].bitcast(F32).rearrange(
                 "p (b c r u) -> p b c r u", b=BATCH, c=PASSES, u=PAIR
@@ -100,30 +106,35 @@ def tile_denseattentiononehead_pa_kernel(tc, hidden_states, W_q, cos, sin, grad_
                     for u in range(PAIR):
                         nc.tensor.transpose(turned[:, c, u, :], words[:, b, c, :, u], identity[:])
                 nc.scalar.copy(out=grouped_words[:, b], in_=turned[:].rearrange("p c u r -> p c r u"))
+            return g_grouped
+
+        def quantise_tokens(g_grouped):
             g_codes = g_stage.tile([P, BATCH * PASSES * P], U32, align_bytes=64)
             g_scales = g_stage.tile([P, BATCH * PASSES * P], U8, align_bytes=64)
             nc.vector.quantize_mx(out=g_codes[:].bitcast(E5M2_X4), scales=g_scales[:], in_=g_grouped[:])
             return g_codes, g_scales
 
-        def multiply(tokens, b, h):
-            g_codes, g_scales = tokens
-            gh_half = gh_pool.tile([P, HALF], F32, tag="gh_half%d" % h)
-            for c in range(PASSES):
-                token_columns = slice((b * PASSES + c) * P, (b * PASSES + c + 1) * P)
-                nc.tensor.matmul_mx(
-                    out=gh_half[:],
-                    lhsT=g_codes[:, token_columns].bitcast(E5M2_X4),
-                    lhsT_scale=g_scales[:, token_columns],
-                    rhs=w_codes[:, c, halves[h]].bitcast(E4M3_X4),
-                    rhs_scale=w_scales[:, c, halves[h]],
-                    start=(c == 0),
-                    stop=(c == PASSES - 1),
-                )
-            return gh_half
+        def multiply(block_tokens, h):
+            g_codes, g_scales = block_tokens
+            gh_halves = []
+            for b in range(BATCH):
+                gh_half = gh_pool.tile([P, HALF], F32, tag="gh_half%d" % h)
+                for c in range(PASSES):
+                    token_columns = slice((b * PASSES + c) * P, (b * PASSES + c + 1) * P)
+                    nc.tensor.matmul_mx(
+                        out=gh_half[:],
+                        lhsT=g_codes[:, token_columns].bitcast(E5M2_X4),
+                        lhsT_scale=g_scales[:, token_columns],
+                        rhs=w_codes[:, c, halves[h]].bitcast(E4M3_X4),
+                        rhs_scale=w_scales[:, c, halves[h]],
+                        start=(c == 0),
+                        stop=(c == PASSES - 1),
+                    )
+                gh_halves.append(gh_half)
+            return gh_halves
 
-        def low_stage(n, tokens):
-            cos_rows, sin_rows = blocks[n][1], blocks[n][2]
-            gh_low = [multiply(tokens, b, 0) for b in range(BATCH)]
+        def start_block(n, gh_low):
+            cos_rows, sin_rows = tables[n]
             by_cos = []
             by_sin = []
             for b in range(BATCH):
@@ -135,33 +146,38 @@ def tile_denseattentiononehead_pa_kernel(tc, hidden_states, W_q, cos, sin, grad_
                 )
             return by_cos, by_sin
 
-        def high_stage(n, tokens, by_cos, by_sin):
-            cos_rows, sin_rows = blocks[n][1], blocks[n][2]
-            gh_high = [multiply(tokens, b, 1) for b in range(BATCH)]
+        def finish_block(n, gh_high, by_cos, by_sin):
+            cos_rows, sin_rows = tables[n]
             for b in range(BATCH):
-                rows = out[b, n * P : (n + 1) * P, :]
                 nc.vector.tensor_tensor(out=by_sin[b][:, low], in0=gh_high[b][:], in1=sin_rows[:, high], op=MULT)
                 nc.vector.tensor_tensor(out=by_cos[b][:, high], in0=gh_high[b][:], in1=cos_rows[:, high], op=MULT)
-                if (n, b) != (L_BLOCKS - 1, BATCH - 1):
+            if n + 1 < L_BLOCKS:
+                for b in range(BATCH):
                     nc.gpsimd.tensor_tensor(out=by_cos[b][:], in0=by_cos[b][:], in1=by_sin[b][:], op=ADD)
-                    nc.sync.dma_start(out=rows, in_=by_cos[b][:])
-                else:
-                    for half in halves:
-                        nc.vector.tensor_tensor(
+                    nc.sync.dma_start(out=out[b, n * P : (n + 1) * P, :], in_=by_cos[b][:])
+            else:
+                adders = (nc.gpsimd, nc.vector)
+                for half in halves:
+                    for b in range(BATCH):
+                        adders[b].tensor_tensor(
                             out=by_cos[b][:, half], in0=by_cos[b][:, half], in1=by_sin[b][:, half], op=ADD
                         )
-                        nc.sync.dma_start(out=rows[:, half], in_=by_cos[b][:, half])
+                        nc.sync.dma_start(out=out[b, n * P : (n + 1) * P, half], in_=by_cos[b][:, half])
 
         quantise_w(0, 0, nc.vector.tensor_copy)
         quantise_w(0, 1, nc.vector.tensor_copy)
-        tokens = quantise_tokens(0)
-        sums = low_stage(0, tokens)
+        grouped = [turn_tokens(0)]
+        tokens = [quantise_tokens(grouped[0])]
+        sums = start_block(0, multiply(tokens[0], 0))
         quantise_w(1, 0, nc.scalar.copy)
         quantise_w(1, 1, nc.vector.tensor_copy)
+        for n in range(1, AHEAD):
+            grouped.append(turn_tokens(n))
         for n in range(L_BLOCKS):
+            if n + AHEAD < L_BLOCKS:
+                grouped.append(turn_tokens(n + AHEAD))
             if n + 1 < L_BLOCKS:
-                next_tokens = quantise_tokens(n + 1)
-            high_stage(n, tokens, *sums)
+                tokens.append(quantise_tokens(grouped[n + 1]))
+            finish_block(n, multiply(tokens[n], 1), *sums)
             if n + 1 < L_BLOCKS:
-                tokens = next_tokens
-                sums = low_stage(n + 1, tokens)
+                sums = start_block(n + 1, multiply(tokens[n + 1], 0))

@@ -37,7 +37,6 @@ def tile_denseattentiononehead_pa_kernel(tc, hidden_states, W_q, cos, sin, grad_
         tc.tile_pool(name="results", bufs=5 * BATCH) as results,
         tc.psum_pool(name="transposed", bufs=2) as transposed,
         tc.psum_pool(name="gh", bufs=3) as gh_pool,
-        tc.manual_schedule(),
     ):
         def load_w(h, c):
             w_tile = resident.tile([P, PACK, HALF], BF16, name="w_rows%d%d" % (h, c))

@@ -19,7 +19,6 @@ PASSES = WIDTH // K_PASS
 L_BLOCKS = LENGTH // P
 PAIR = 2
 RUN = 4
-AHEAD = 2
 
 FLOPS = 2 * BATCH * LENGTH * WIDTH * WIDTH
 BYTES = 2 * (BATCH * LENGTH * WIDTH + 3 * WIDTH * WIDTH) + 4 * BATCH * LENGTH * WIDTH
@@ -29,14 +28,16 @@ def tile_denseattentiononehead_pa_kernel(tc, hidden_states, W_q, cos, sin, grad_
     nc = tc.nc
     low, high = slice(0, HALF), slice(HALF, WIDTH)
     halves = (low, high)
+    tiles = [(n, b) for n in range(L_BLOCKS) for b in range(BATCH)]
     with (
         tc.tile_pool(name="resident", bufs=1) as resident,
         tc.tile_pool(name="w_stage", bufs=PASSES * 2) as w_stage,
-        tc.tile_pool(name="g_stage", bufs=AHEAD + 2) as g_stage,
-        tc.tile_pool(name="products", bufs=3 * BATCH) as products,
-        tc.tile_pool(name="results", bufs=5 * BATCH) as results,
+        tc.tile_pool(name="g_stage", bufs=4) as g_stage,
+        tc.tile_pool(name="products", bufs=4) as products,
+        tc.tile_pool(name="results", bufs=8) as results,
         tc.psum_pool(name="transposed", bufs=2) as transposed,
         tc.psum_pool(name="gh", bufs=3) as gh_pool,
+        tc.manual_schedule(),
     ):
         def load_w(h, c):
             w_tile = resident.tile([P, PACK, HALF], BF16, name="w_rows%d%d" % (h, c))
@@ -46,34 +47,27 @@ def tile_denseattentiononehead_pa_kernel(tc, hidden_states, W_q, cos, sin, grad_
             )
             return w_tile
 
-        def load_tokens(n):
+        def load_block(n):
+            positions = slice(n * P, (n + 1) * P)
             g_tile = resident.tile([P, BATCH * WIDTH], BF16, name="g_rows%d" % n)
             nc.sync.dma_start(
                 out=g_tile[:].rearrange("p (b o) -> p b o", b=BATCH),
-                in_=grad_out[:, n * P : (n + 1) * P, :].rearrange("b p o -> p b o"),
+                in_=grad_out[:, positions, :].rearrange("b p o -> p b o"),
             )
-            return g_tile
-
-        def load_tables(n):
+            if n == 0:
+                for c in range(PASSES):
+                    w_rows[(0, c)] = load_w(0, c)
             cos_tile = resident.tile([P, WIDTH], BF16, name="cos_rows%d" % n)
-            nc.sync.dma_start(out=cos_tile[:], in_=cos[n * P : (n + 1) * P, :])
+            nc.sync.dma_start(out=cos_tile[:], in_=cos[positions, :])
             sin_tile = resident.tile([P, WIDTH], BF16, name="sin_rows%d" % n)
-            nc.sync.dma_start(out=sin_tile[:], in_=sin[n * P : (n + 1) * P, :])
-            return cos_tile, sin_tile
+            nc.sync.dma_start(out=sin_tile[:], in_=sin[positions, :])
+            if n == 0:
+                for c in range(PASSES):
+                    w_rows[(1, c)] = load_w(1, c)
+            return g_tile, cos_tile, sin_tile
 
-        g_rows = [load_tokens(0)]
         w_rows = {}
-        for c in range(PASSES):
-            w_rows[(0, c)] = load_w(0, c)
-        tables = [load_tables(0)]
-        for c in range(PASSES):
-            w_rows[(1, c)] = load_w(1, c)
-        for n in range(1, AHEAD):
-            g_rows.append(load_tokens(n))
-        for n in range(1, L_BLOCKS):
-            if n + AHEAD - 1 < L_BLOCKS:
-                g_rows.append(load_tokens(n + AHEAD - 1))
-            tables.append(load_tables(n))
+        blocks = [load_block(n) for n in range(L_BLOCKS)]
 
         identity = resident.tile([P, P], F32, name="identity")
         make_identity(nc, identity[:])
@@ -81,102 +75,96 @@ def tile_denseattentiononehead_pa_kernel(tc, hidden_states, W_q, cos, sin, grad_
         w_codes = resident.tile([P, PASSES, WIDTH], U32, name="w_codes", align_bytes=64)
         w_scales = resident.tile([P, PASSES, WIDTH], U8, name="w_scales", align_bytes=64)
 
-        def quantise_w(h, c, regroup):
+        def regroup_w(h, c, copy):
             w_grouped = w_stage.tile([P, HALF * PACK], BF16, align_bytes=64)
-            regroup(
+            copy(
                 out=w_grouped[:].rearrange("p (m i t) -> p m t i", i=RUN, t=PACK),
                 in_=w_rows[(h, c)][:].rearrange("p t (m i) -> p m t i", i=RUN),
             )
+            return w_grouped
+
+        def quantise_w(h, c, w_grouped):
             nc.vector.quantize_mx(
                 out=w_codes[:, c, halves[h]].bitcast(E4M3_X4),
                 scales=w_scales[:, c, halves[h]],
                 in_=w_grouped[:],
             )
 
-        def turn_tokens(n):
-            words = g_rows[n][:].bitcast(F32).rearrange("p (b c q u) -> p b c q u", b=BATCH, c=PASSES, u=PAIR)
-            g_grouped = g_stage.tile([P, BATCH * PASSES * P * PACK], BF16, align_bytes=64)
-            grouped_words = g_grouped[:].bitcast(F32).rearrange(
-                "p (b c r u) -> p b c r u", b=BATCH, c=PASSES, u=PAIR
+        def turn_tokens(i):
+            n, b = tiles[i]
+            words = blocks[n][0][:].bitcast(F32).rearrange("p (b c q u) -> p b c q u", b=BATCH, c=PASSES, u=PAIR)
+            turned = transposed.tile([P, PASSES, PAIR, P], F32)
+            for c in range(PASSES):
+                for u in range(PAIR):
+                    nc.tensor.transpose(turned[:, c, u, :], words[:, b, c, :, u], identity[:])
+            g_grouped = g_stage.tile([P, PASSES * P * PACK], BF16, align_bytes=64)
+            nc.scalar.copy(
+                out=g_grouped[:].bitcast(F32).rearrange("p (c r u) -> p c r u", c=PASSES, u=PAIR),
+                in_=turned[:].rearrange("p c u r -> p c r u"),
             )
-            for b in range(BATCH):
-                turned = transposed.tile([P, PASSES, PAIR, P], F32)
-                for c in range(PASSES):
-                    for u in range(PAIR):
-                        nc.tensor.transpose(turned[:, c, u, :], words[:, b, c, :, u], identity[:])
-                nc.scalar.copy(out=grouped_words[:, b], in_=turned[:].rearrange("p c u r -> p c r u"))
             return g_grouped
 
         def quantise_tokens(g_grouped):
-            g_codes = g_stage.tile([P, BATCH * PASSES * P], U32, align_bytes=64)
-            g_scales = g_stage.tile([P, BATCH * PASSES * P], U8, align_bytes=64)
+            g_codes = g_stage.tile([P, PASSES * P], U32, align_bytes=64)
+            g_scales = g_stage.tile([P, PASSES * P], U8, align_bytes=64)
             nc.vector.quantize_mx(out=g_codes[:].bitcast(E5M2_X4), scales=g_scales[:], in_=g_grouped[:])
             return g_codes, g_scales
 
-        def multiply(block_tokens, h):
-            g_codes, g_scales = block_tokens
-            gh_halves = []
-            for b in range(BATCH):
-                gh_half = gh_pool.tile([P, HALF], F32, tag="gh_half%d" % h)
-                for c in range(PASSES):
-                    token_columns = slice((b * PASSES + c) * P, (b * PASSES + c + 1) * P)
-                    nc.tensor.matmul_mx(
-                        out=gh_half[:],
-                        lhsT=g_codes[:, token_columns].bitcast(E5M2_X4),
-                        lhsT_scale=g_scales[:, token_columns],
-                        rhs=w_codes[:, c, halves[h]].bitcast(E4M3_X4),
-                        rhs_scale=w_scales[:, c, halves[h]],
-                        start=(c == 0),
-                        stop=(c == PASSES - 1),
-                    )
-                gh_halves.append(gh_half)
-            return gh_halves
-
-        def start_block(n, gh_low):
-            cos_rows, sin_rows = tables[n]
-            by_cos = []
-            by_sin = []
-            for b in range(BATCH):
-                by_cos.append(results.tile([P, WIDTH], F32, name="by_cos", tag="by_cos"))
-                by_sin.append(products.tile([P, WIDTH], F32, name="by_sin", tag="by_sin"))
-                nc.vector.tensor_tensor(out=by_cos[b][:, low], in0=gh_low[b][:], in1=cos_rows[:, low], op=MULT)
-                nc.vector.scalar_tensor_tensor(
-                    out=by_sin[b][:, high], in0=gh_low[b][:], scalar=-1.0, in1=sin_rows[:, low], op0=MULT, op1=MULT
+        def multiply(tile_tokens, h):
+            g_codes, g_scales = tile_tokens
+            gh_half = gh_pool.tile([P, HALF], F32, tag="gh_half%d" % h)
+            for c in range(PASSES):
+                nc.tensor.matmul_mx(
+                    out=gh_half[:],
+                    lhsT=g_codes[:, c * P : (c + 1) * P].bitcast(E5M2_X4),
+                    lhsT_scale=g_scales[:, c * P : (c + 1) * P],
+                    rhs=w_codes[:, c, halves[h]].bitcast(E4M3_X4),
+                    rhs_scale=w_scales[:, c, halves[h]],
+                    start=(c == 0),
+                    stop=(c == PASSES - 1),
                 )
+            return gh_half
+
+        def low_products(i, gh_low):
+            cos_rows, sin_rows = blocks[tiles[i][0]][1:]
+            by_cos = results.tile([P, WIDTH], F32)
+            by_sin = products.tile([P, WIDTH], F32)
+            nc.vector.tensor_tensor(out=by_cos[:, low], in0=gh_low[:], in1=cos_rows[:, low], op=MULT)
+            nc.vector.scalar_tensor_tensor(
+                out=by_sin[:, high], in0=gh_low[:], scalar=-1.0, in1=sin_rows[:, low], op0=MULT, op1=MULT
+            )
             return by_cos, by_sin
 
-        def finish_block(n, gh_high, by_cos, by_sin):
-            cos_rows, sin_rows = tables[n]
-            for b in range(BATCH):
-                nc.vector.tensor_tensor(out=by_sin[b][:, low], in0=gh_high[b][:], in1=sin_rows[:, high], op=MULT)
-                nc.vector.tensor_tensor(out=by_cos[b][:, high], in0=gh_high[b][:], in1=cos_rows[:, high], op=MULT)
-            if n + 1 < L_BLOCKS:
-                for b in range(BATCH):
-                    nc.gpsimd.tensor_tensor(out=by_cos[b][:], in0=by_cos[b][:], in1=by_sin[b][:], op=ADD)
-                    nc.sync.dma_start(out=out[b, n * P : (n + 1) * P, :], in_=by_cos[b][:])
+        def high_products_sum_and_store(i, gh_high, by_cos, by_sin):
+            n, b = tiles[i]
+            cos_rows, sin_rows = blocks[n][1:]
+            rows = out[b, n * P : (n + 1) * P, :]
+            nc.vector.tensor_tensor(out=by_sin[:, low], in0=gh_high[:], in1=sin_rows[:, high], op=MULT)
+            nc.vector.tensor_tensor(out=by_cos[:, high], in0=gh_high[:], in1=cos_rows[:, high], op=MULT)
+            if i + 1 < len(tiles):
+                nc.gpsimd.tensor_tensor(out=by_cos[:], in0=by_cos[:], in1=by_sin[:], op=ADD)
+                nc.sync.dma_start(out=rows, in_=by_cos[:])
             else:
-                adders = (nc.gpsimd, nc.vector)
                 for half in halves:
-                    for b in range(BATCH):
-                        adders[b].tensor_tensor(
-                            out=by_cos[b][:, half], in0=by_cos[b][:, half], in1=by_sin[b][:, half], op=ADD
-                        )
-                        nc.sync.dma_start(out=out[b, n * P : (n + 1) * P, half], in_=by_cos[b][:, half])
+                    nc.vector.tensor_tensor(out=by_cos[:, half], in0=by_cos[:, half], in1=by_sin[:, half], op=ADD)
+                    nc.sync.dma_start(out=rows[:, half], in_=by_cos[:, half])
 
-        quantise_w(0, 0, nc.vector.tensor_copy)
-        quantise_w(0, 1, nc.vector.tensor_copy)
-        grouped = [turn_tokens(0)]
-        tokens = [quantise_tokens(grouped[0])]
-        sums = start_block(0, multiply(tokens[0], 0))
-        quantise_w(1, 0, nc.scalar.copy)
-        quantise_w(1, 1, nc.vector.tensor_copy)
-        for n in range(1, AHEAD):
-            grouped.append(turn_tokens(n))
-        for n in range(L_BLOCKS):
-            if n + AHEAD < L_BLOCKS:
-                grouped.append(turn_tokens(n + AHEAD))
-            if n + 1 < L_BLOCKS:
-                tokens.append(quantise_tokens(grouped[n + 1]))
-            finish_block(n, multiply(tokens[n], 1), *sums)
-            if n + 1 < L_BLOCKS:
-                sums = start_block(n + 1, multiply(tokens[n + 1], 0))
+        w_low = [regroup_w(0, c, nc.vector.tensor_copy) for c in range(PASSES)]
+        for c in range(PASSES):
+            quantise_w(0, c, w_low[c])
+        grouped = [turn_tokens(0), turn_tokens(1)]
+        tokens = [quantise_tokens(grouped[0]), quantise_tokens(grouped[1])]
+        sums = low_products(0, multiply(tokens[0], 0))
+        w_high = [regroup_w(1, 0, nc.scalar.copy), regroup_w(1, 1, nc.vector.tensor_copy)]
+        grouped.append(turn_tokens(2))
+        for c in range(PASSES):
+            quantise_w(1, c, w_high[c])
+
+        for i in range(len(tiles)):
+            high_products_sum_and_store(i, multiply(tokens[i], 1), *sums)
+            if i + 3 < len(tiles):
+                grouped.append(turn_tokens(i + 3))
+            if i + 2 < len(tiles):
+                tokens.append(quantise_tokens(grouped[i + 2]))
+            if i + 1 < len(tiles):
+                sums = low_products(i + 1, multiply(tokens[i + 1], 0))

@@ -18,6 +18,7 @@ K_PASS = P * PACK
 PASSES = WIDTH // K_PASS
 L_BLOCKS = LENGTH // P
 PAIR = 2
+VECTOR_COLS = 352
 RUN = 4
 
 FLOPS = 2 * BATCH * LENGTH * WIDTH * WIDTH
@@ -47,27 +48,32 @@ def tile_denseattentiononehead_pa_kernel(tc, hidden_states, W_q, cos, sin, grad_
             )
             return w_tile
 
-        def load_block(n):
-            positions = slice(n * P, (n + 1) * P)
-            g_tile = resident.tile([P, BATCH * WIDTH], BF16, name="g_rows%d" % n)
+        def load_tokens(n, g_tile, batches):
+            b0, b1 = batches[0], batches[-1] + 1
             nc.sync.dma_start(
-                out=g_tile[:].rearrange("p (b o) -> p b o", b=BATCH),
-                in_=grad_out[:, positions, :].rearrange("b p o -> p b o"),
+                out=g_tile[:, b0 * WIDTH : b1 * WIDTH].rearrange("p (b o) -> p b o", b=b1 - b0),
+                in_=grad_out[b0:b1, n * P : (n + 1) * P, :].rearrange("b p o -> p b o"),
             )
-            if n == 0:
-                for c in range(PASSES):
-                    w_rows[(0, c)] = load_w(0, c)
-            cos_tile = resident.tile([P, WIDTH], BF16, name="cos_rows%d" % n)
-            nc.sync.dma_start(out=cos_tile[:], in_=cos[positions, :])
-            sin_tile = resident.tile([P, WIDTH], BF16, name="sin_rows%d" % n)
-            nc.sync.dma_start(out=sin_tile[:], in_=sin[positions, :])
-            if n == 0:
-                for c in range(PASSES):
-                    w_rows[(1, c)] = load_w(1, c)
-            return g_tile, cos_tile, sin_tile
 
+        def load_table(table, n, name):
+            table_tile = resident.tile([P, WIDTH], BF16, name="%s_rows%d" % (name, n))
+            nc.sync.dma_start(out=table_tile[:], in_=table[n * P : (n + 1) * P, :])
+            return table_tile
+
+        g_rows = [resident.tile([P, BATCH * WIDTH], BF16, name="g_rows%d" % n) for n in range(L_BLOCKS)]
         w_rows = {}
-        blocks = [load_block(n) for n in range(L_BLOCKS)]
+        blocks = []
+        for c in range(PASSES):
+            w_rows[(0, c)] = load_w(0, c)
+        load_tokens(0, g_rows[0], (0,))
+        for c in range(PASSES):
+            w_rows[(1, c)] = load_w(1, c)
+        for n in range(L_BLOCKS):
+            if n > 0:
+                load_tokens(n, g_rows[n], (0, 1))
+            blocks.append((g_rows[n], load_table(cos, n, "cos"), load_table(sin, n, "sin")))
+            if n == 0:
+                load_tokens(0, g_rows[0], (1,))
 
         identity = resident.tile([P, P], F32, name="identity")
         make_identity(nc, identity[:])
@@ -75,12 +81,13 @@ def tile_denseattentiononehead_pa_kernel(tc, hidden_states, W_q, cos, sin, grad_
         w_codes = resident.tile([P, PASSES, WIDTH], U32, name="w_codes", align_bytes=64)
         w_scales = resident.tile([P, PASSES, WIDTH], U8, name="w_scales", align_bytes=64)
 
-        def regroup_w(h, c, copy):
+        def regroup_w(h, c):
             w_grouped = w_stage.tile([P, HALF * PACK], BF16, align_bytes=64)
-            copy(
-                out=w_grouped[:].rearrange("p (m i t) -> p m t i", i=RUN, t=PACK),
-                in_=w_rows[(h, c)][:].rearrange("p t (m i) -> p m t i", i=RUN),
-            )
+            for copy, cols in ((nc.vector.tensor_copy, slice(0, VECTOR_COLS)), (nc.scalar.copy, slice(VECTOR_COLS, HALF))):
+                copy(
+                    out=w_grouped[:, cols.start * PACK : cols.stop * PACK].rearrange("p (m i t) -> p m t i", i=RUN, t=PACK),
+                    in_=w_rows[(h, c)][:, :, cols].rearrange("p t (m i) -> p m t i", i=RUN),
+                )
             return w_grouped
 
         def quantise_w(h, c, w_grouped):
@@ -149,19 +156,23 @@ def tile_denseattentiononehead_pa_kernel(tc, hidden_states, W_q, cos, sin, grad_
                     nc.vector.tensor_tensor(out=by_cos[:, half], in0=by_cos[:, half], in1=by_sin[:, half], op=ADD)
                     nc.sync.dma_start(out=rows[:, half], in_=by_cos[:, half])
 
-        w_low = [regroup_w(0, c, nc.vector.tensor_copy) for c in range(PASSES)]
+        w_low = [regroup_w(0, c) for c in range(PASSES)]
         for c in range(PASSES):
             quantise_w(0, c, w_low[c])
-        grouped = [turn_tokens(0), turn_tokens(1)]
-        tokens = [quantise_tokens(grouped[0]), quantise_tokens(grouped[1])]
-        sums = low_products(0, multiply(tokens[0], 0))
-        w_high = [regroup_w(1, 0, nc.scalar.copy), regroup_w(1, 1, nc.vector.tensor_copy)]
-        grouped.append(turn_tokens(2))
+        grouped = [turn_tokens(0)]
+        w_high = [regroup_w(1, 0)]
+        tokens = [quantise_tokens(grouped[0])]
+        w_high.append(regroup_w(1, 1))
         for c in range(PASSES):
             quantise_w(1, c, w_high[c])
+        sums = low_products(0, multiply(tokens[0], 0))
+        grouped.append(turn_tokens(1))
+        tokens.append(quantise_tokens(grouped[1]))
+        gh_high = multiply(tokens[0], 1)
+        grouped.append(turn_tokens(2))
 
         for i in range(len(tiles)):
-            high_products_sum_and_store(i, multiply(tokens[i], 1), *sums)
+            high_products_sum_and_store(i, gh_high if i == 0 else multiply(tokens[i], 1), *sums)
             if i + 3 < len(tiles):
                 grouped.append(turn_tokens(i + 3))
             if i + 2 < len(tiles):

@@ -55,25 +55,31 @@ def tile_denseattentiononehead_pa_kernel(tc, hidden_states, W_q, cos, sin, grad_
                 in_=grad_out[b0:b1, n * P : (n + 1) * P, :].rearrange("b p o -> p b o"),
             )
 
-        def load_table(table, n, name):
-            table_tile = resident.tile([P, WIDTH], BF16, name="%s_rows%d" % (name, n))
-            nc.sync.dma_start(out=table_tile[:], in_=table[n * P : (n + 1) * P, :])
-            return table_tile
+        def load_table(table, table_tile, n, cols):
+            nc.sync.dma_start(out=table_tile[:, cols], in_=table[n * P : (n + 1) * P, cols])
 
         g_rows = [resident.tile([P, BATCH * WIDTH], BF16, name="g_rows%d" % n) for n in range(L_BLOCKS)]
+        cos_rows = [resident.tile([P, WIDTH], BF16, name="cos_rows%d" % n) for n in range(L_BLOCKS)]
+        sin_rows = [resident.tile([P, WIDTH], BF16, name="sin_rows%d" % n) for n in range(L_BLOCKS)]
+        blocks = [(g_rows[n], cos_rows[n], sin_rows[n]) for n in range(L_BLOCKS)]
         w_rows = {}
-        blocks = []
         for c in range(PASSES):
             w_rows[(0, c)] = load_w(0, c)
         load_tokens(0, g_rows[0], (0,))
         for c in range(PASSES):
             w_rows[(1, c)] = load_w(1, c)
-        for n in range(L_BLOCKS):
-            if n > 0:
-                load_tokens(n, g_rows[n], (0, 1))
-            blocks.append((g_rows[n], load_table(cos, n, "cos"), load_table(sin, n, "sin")))
-            if n == 0:
-                load_tokens(0, g_rows[0], (1,))
+        load_table(cos, cos_rows[0], 0, low)
+        load_table(sin, sin_rows[0], 0, low)
+        load_tokens(0, g_rows[0], (1,))
+        load_tokens(1, g_rows[1], (0,))
+        load_table(sin, sin_rows[0], 0, high)
+        load_table(cos, cos_rows[0], 0, high)
+        load_tokens(1, g_rows[1], (1,))
+        for n in range(1, L_BLOCKS):
+            if n + 1 < L_BLOCKS:
+                load_tokens(n + 1, g_rows[n + 1], (0, 1))
+            load_table(cos, cos_rows[n], n, slice(0, WIDTH))
+            load_table(sin, sin_rows[n], n, slice(0, WIDTH))
 
         identity = resident.tile([P, P], F32, name="identity")
         make_identity(nc, identity[:])
@@ -142,11 +148,13 @@ def tile_denseattentiononehead_pa_kernel(tc, hidden_states, W_q, cos, sin, grad_
             )
             return by_cos, by_sin
 
-        def high_products_sum_and_store(i, gh_high, by_cos, by_sin):
+        def high_products_sum_and_store(i, gh_high, by_cos, by_sin, between=None):
             n, b = tiles[i]
             cos_rows, sin_rows = blocks[n][1:]
             rows = out[b, n * P : (n + 1) * P, :]
             nc.vector.tensor_tensor(out=by_sin[:, low], in0=gh_high[:], in1=sin_rows[:, high], op=MULT)
+            if between is not None:
+                between()
             nc.vector.tensor_tensor(out=by_cos[:, high], in0=gh_high[:], in1=cos_rows[:, high], op=MULT)
             if i + 1 < len(tiles):
                 nc.gpsimd.tensor_tensor(out=by_cos[:], in0=by_cos[:], in1=by_sin[:], op=ADD)
@@ -172,10 +180,13 @@ def tile_denseattentiononehead_pa_kernel(tc, hidden_states, W_q, cos, sin, grad_
         grouped.append(turn_tokens(2))
 
         for i in range(len(tiles)):
-            high_products_sum_and_store(i, gh_high if i == 0 else multiply(tokens[i], 1), *sums)
-            if i + 3 < len(tiles):
-                grouped.append(turn_tokens(i + 3))
-            if i + 2 < len(tiles):
-                tokens.append(quantise_tokens(grouped[i + 2]))
+            if i == 0:
+                high_products_sum_and_store(0, gh_high, *sums, between=lambda: tokens.append(quantise_tokens(grouped[2])))
+            else:
+                high_products_sum_and_store(i, multiply(tokens[i], 1), *sums)
+                if i + 2 < len(tiles):
+                    tokens.append(quantise_tokens(grouped[i + 2]))
             if i + 1 < len(tiles):
                 sums = low_products(i + 1, multiply(tokens[i + 1], 0))
+            if i + 3 < len(tiles):
+                grouped.append(turn_tokens(i + 3))

@@ -19,6 +19,7 @@ PASSES = WIDTH // K_PASS
 L_BLOCKS = LENGTH // P
 PAIR = 2
 VECTOR_COLS = 352
+SLOTS = 4
 RUN = 4
 
 FLOPS = 2 * BATCH * LENGTH * WIDTH * WIDTH
@@ -34,7 +35,6 @@ def tile_denseattentiononehead_pa_kernel(tc, hidden_states, W_q, cos, sin, grad_
         tc.tile_pool(name="resident", bufs=1) as resident,
         tc.tile_pool(name="w_stage", bufs=PASSES * 2) as w_stage,
         tc.tile_pool(name="g_stage", bufs=4) as g_stage,
-        tc.tile_pool(name="products", bufs=4) as products,
         tc.tile_pool(name="results", bufs=8) as results,
         tc.psum_pool(name="transposed", bufs=2) as transposed,
         tc.psum_pool(name="gh", bufs=3) as gh_pool,
@@ -55,31 +55,42 @@ def tile_denseattentiononehead_pa_kernel(tc, hidden_states, W_q, cos, sin, grad_
                 in_=grad_out[b0:b1, n * P : (n + 1) * P, :].rearrange("b p o -> p b o"),
             )
 
-        def load_table(table, table_tile, n, cols):
-            nc.sync.dma_start(out=table_tile[:, cols], in_=table[n * P : (n + 1) * P, cols])
+        def slot(s0, s1):
+            return slice(s0 * HALF, s1 * HALF)
+
+        def load_slot(table, n, s, half):
+            nc.sync.dma_start(out=tables[n][:, slot(s, s + 1)], in_=table[n * P : (n + 1) * P, half])
+
+        def load_tables(n):
+            positions = slice(n * P, (n + 1) * P)
+            nc.sync.dma_start(
+                out=tables[n][:].rearrange("p (s j) -> p s j", s=SLOTS)[:, 0 : SLOTS : SLOTS - 1, :],
+                in_=cos[positions, :].rearrange("p (h j) -> p h j", h=2),
+            )
+            nc.sync.dma_start(out=tables[n][:, slot(1, 3)], in_=sin[positions, :])
+
+        def negate_sin_low(n):
+            nc.scalar.mul(out=tables[n][:, slot(1, 2)], in_=tables[n][:, slot(1, 2)], mul=-1.0)
 
         g_rows = [resident.tile([P, BATCH * WIDTH], BF16, name="g_rows%d" % n) for n in range(L_BLOCKS)]
-        cos_rows = [resident.tile([P, WIDTH], BF16, name="cos_rows%d" % n) for n in range(L_BLOCKS)]
-        sin_rows = [resident.tile([P, WIDTH], BF16, name="sin_rows%d" % n) for n in range(L_BLOCKS)]
-        blocks = [(g_rows[n], cos_rows[n], sin_rows[n]) for n in range(L_BLOCKS)]
+        tables = [resident.tile([P, SLOTS * HALF], BF16, name="tables%d" % n) for n in range(L_BLOCKS)]
         w_rows = {}
         for c in range(PASSES):
             w_rows[(0, c)] = load_w(0, c)
         load_tokens(0, g_rows[0], (0,))
         for c in range(PASSES):
             w_rows[(1, c)] = load_w(1, c)
-        load_table(cos, cos_rows[0], 0, low)
-        load_table(sin, sin_rows[0], 0, low)
+        load_slot(sin, 0, 1, low)
+        load_slot(cos, 0, 0, low)
         load_tokens(0, g_rows[0], (1,))
         load_tokens(1, g_rows[1], (0,))
-        load_table(sin, sin_rows[0], 0, high)
-        load_table(cos, cos_rows[0], 0, high)
+        load_slot(sin, 0, 2, high)
+        load_slot(cos, 0, 3, high)
         load_tokens(1, g_rows[1], (1,))
         for n in range(1, L_BLOCKS):
             if n + 1 < L_BLOCKS:
                 load_tokens(n + 1, g_rows[n + 1], (0, 1))
-            load_table(cos, cos_rows[n], n, slice(0, WIDTH))
-            load_table(sin, sin_rows[n], n, slice(0, WIDTH))
+            load_tables(n)
 
         identity = resident.tile([P, P], F32, name="identity")
         make_identity(nc, identity[:])
@@ -105,7 +116,7 @@ def tile_denseattentiononehead_pa_kernel(tc, hidden_states, W_q, cos, sin, grad_
 
         def turn_tokens(i):
             n, b = tiles[i]
-            words = blocks[n][0][:].bitcast(F32).rearrange("p (b c q u) -> p b c q u", b=BATCH, c=PASSES, u=PAIR)
+            words = g_rows[n][:].bitcast(F32).rearrange("p (b c q u) -> p b c q u", b=BATCH, c=PASSES, u=PAIR)
             turned = transposed.tile([P, PASSES, PAIR, P], F32)
             for c in range(PASSES):
                 for u in range(PAIR):
@@ -138,31 +149,32 @@ def tile_denseattentiononehead_pa_kernel(tc, hidden_states, W_q, cos, sin, grad_
                 )
             return gh_half
 
-        def low_products(i, gh_low):
-            cos_rows, sin_rows = blocks[tiles[i][0]][1:]
-            by_cos = results.tile([P, WIDTH], F32)
-            by_sin = products.tile([P, WIDTH], F32)
-            nc.vector.tensor_tensor(out=by_cos[:, low], in0=gh_low[:], in1=cos_rows[:, low], op=MULT)
-            nc.vector.scalar_tensor_tensor(
-                out=by_sin[:, high], in0=gh_low[:], scalar=-1.0, in1=sin_rows[:, low], op0=MULT, op1=MULT
+        def products(i, gh_half, terms, h):
+            nc.vector.tensor_tensor(
+                out=terms[:, slot(2 * h, 2 * h + 2)].rearrange("p (s j) -> p s j", s=2),
+                in0=gh_half[:].unsqueeze(1).to_broadcast([P, 2, HALF]),
+                in1=tables[tiles[i][0]][:, slot(2 * h, 2 * h + 2)].rearrange("p (s j) -> p s j", s=2),
+                op=MULT,
             )
-            return by_cos, by_sin
 
-        def high_products_sum_and_store(i, gh_high, by_cos, by_sin, between=None):
+        def low_products(i, gh_low):
+            terms = results.tile([P, SLOTS * HALF], F32)
+            products(i, gh_low, terms, 0)
+            return terms
+
+        def high_products_sum_and_store(i, gh_high, terms):
             n, b = tiles[i]
-            cos_rows, sin_rows = blocks[n][1:]
             rows = out[b, n * P : (n + 1) * P, :]
-            nc.vector.tensor_tensor(out=by_sin[:, low], in0=gh_high[:], in1=sin_rows[:, high], op=MULT)
-            if between is not None:
-                between()
-            nc.vector.tensor_tensor(out=by_cos[:, high], in0=gh_high[:], in1=cos_rows[:, high], op=MULT)
+            products(i, gh_high, terms, 1)
             if i + 1 < len(tiles):
-                nc.gpsimd.tensor_tensor(out=by_cos[:], in0=by_cos[:], in1=by_sin[:], op=ADD)
-                nc.sync.dma_start(out=rows, in_=by_cos[:])
+                nc.gpsimd.tensor_tensor(out=terms[:, slot(0, 2)], in0=terms[:, slot(0, 2)], in1=terms[:, slot(2, 4)], op=ADD)
+                nc.sync.dma_start(out=rows, in_=terms[:, slot(0, 2)])
             else:
-                for half in halves:
-                    nc.vector.tensor_tensor(out=by_cos[:, half], in0=by_cos[:, half], in1=by_sin[:, half], op=ADD)
-                    nc.sync.dma_start(out=rows[:, half], in_=by_cos[:, half])
+                for s in range(2):
+                    nc.vector.tensor_tensor(
+                        out=terms[:, slot(s, s + 1)], in0=terms[:, slot(s, s + 1)], in1=terms[:, slot(s + 2, s + 3)], op=ADD
+                    )
+                    nc.sync.dma_start(out=rows[:, halves[s]], in_=terms[:, slot(s, s + 1)])
 
         w_low = [regroup_w(0, c) for c in range(PASSES)]
         for c in range(PASSES):
@@ -171,22 +183,23 @@ def tile_denseattentiononehead_pa_kernel(tc, hidden_states, W_q, cos, sin, grad_
         w_high = [regroup_w(1, 0)]
         tokens = [quantise_tokens(grouped[0])]
         w_high.append(regroup_w(1, 1))
+        negate_sin_low(0)
         for c in range(PASSES):
             quantise_w(1, c, w_high[c])
-        sums = low_products(0, multiply(tokens[0], 0))
+        terms = low_products(0, multiply(tokens[0], 0))
         grouped.append(turn_tokens(1))
+        grouped.append(turn_tokens(2))
         tokens.append(quantise_tokens(grouped[1]))
         gh_high = multiply(tokens[0], 1)
-        grouped.append(turn_tokens(2))
+        tokens.append(quantise_tokens(grouped[2]))
 
         for i in range(len(tiles)):
-            if i == 0:
-                high_products_sum_and_store(0, gh_high, *sums, between=lambda: tokens.append(quantise_tokens(grouped[2])))
-            else:
-                high_products_sum_and_store(i, multiply(tokens[i], 1), *sums)
-                if i + 2 < len(tiles):
-                    tokens.append(quantise_tokens(grouped[i + 2]))
+            high_products_sum_and_store(i, gh_high if i == 0 else multiply(tokens[i], 1), terms)
+            if 0 < i and i + 2 < len(tiles):
+                tokens.append(quantise_tokens(grouped[i + 2]))
             if i + 1 < len(tiles):
-                sums = low_products(i + 1, multiply(tokens[i + 1], 0))
+                terms = low_products(i + 1, multiply(tokens[i + 1], 0))
             if i + 3 < len(tiles):
                 grouped.append(turn_tokens(i + 3))
+            if i % BATCH == 0 and i // BATCH + 1 < L_BLOCKS:
+                negate_sin_low(i // BATCH + 1)

@@ -20,6 +20,7 @@ L_BLOCKS = LENGTH // P
 PAIR = 2
 VECTOR_COLS = 352
 SLOTS = 4
+GPSIMD_COLS = 896
 RUN = 4
 
 FLOPS = 2 * BATCH * LENGTH * WIDTH * WIDTH
@@ -117,7 +118,7 @@ def tile_denseattentiononehead_pa_kernel(tc, hidden_states, W_q, cos, sin, grad_
         def turn_tokens(i):
             n, b = tiles[i]
             words = g_rows[n][:].bitcast(F32).rearrange("p (b c q u) -> p b c q u", b=BATCH, c=PASSES, u=PAIR)
-            turned = transposed.tile([P, PASSES, PAIR, P], F32)
+            turned = transposed.tile([P, PASSES, PAIR, P], F32, tag="turned")
             for c in range(PASSES):
                 for u in range(PAIR):
                     nc.tensor.transpose(turned[:, c, u, :], words[:, b, c, :, u], identity[:])
@@ -162,19 +163,31 @@ def tile_denseattentiononehead_pa_kernel(tc, hidden_states, W_q, cos, sin, grad_
             products(i, gh_low, terms, 0)
             return terms
 
-        def high_products_sum_and_store(i, gh_high, terms):
+        def sum_on_gpsimd(terms):
+            nc.gpsimd.tensor_tensor(
+                out=terms[:, 0:GPSIMD_COLS],
+                in0=terms[:, 0:GPSIMD_COLS],
+                in1=terms[:, WIDTH : WIDTH + GPSIMD_COLS],
+                op=ADD,
+            )
+
+        def sum_on_tensor_and_store(i, terms):
             n, b = tiles[i]
-            rows = out[b, n * P : (n + 1) * P, :]
-            products(i, gh_high, terms, 1)
-            if i + 1 < len(tiles):
-                nc.gpsimd.tensor_tensor(out=terms[:, slot(0, 2)], in0=terms[:, slot(0, 2)], in1=terms[:, slot(2, 4)], op=ADD)
-                nc.sync.dma_start(out=rows, in_=terms[:, slot(0, 2)])
-            else:
-                for s in range(2):
-                    nc.vector.tensor_tensor(
-                        out=terms[:, slot(s, s + 1)], in0=terms[:, slot(s, s + 1)], in1=terms[:, slot(s + 2, s + 3)], op=ADD
-                    )
-                    nc.sync.dma_start(out=rows[:, halves[s]], in_=terms[:, slot(s, s + 1)])
+            summed = transposed.tile([P, WIDTH - GPSIMD_COLS], F32, tag="turned")
+            nc.tensor.matmul(out=summed[:], lhsT=identity[:], rhs=terms[:, GPSIMD_COLS:WIDTH], start=True, stop=False)
+            nc.tensor.matmul(
+                out=summed[:], lhsT=identity[:], rhs=terms[:, WIDTH + GPSIMD_COLS : 2 * WIDTH], start=False, stop=True
+            )
+            nc.scalar.copy(out=terms[:, GPSIMD_COLS:WIDTH], in_=summed[:])
+            nc.sync.dma_start(out=out[b, n * P : (n + 1) * P, :], in_=terms[:, 0:WIDTH])
+
+        def sum_on_vector_and_store(i, terms):
+            n, b = tiles[i]
+            for s in range(2):
+                nc.vector.tensor_tensor(
+                    out=terms[:, slot(s, s + 1)], in0=terms[:, slot(s, s + 1)], in1=terms[:, slot(s + 2, s + 3)], op=ADD
+                )
+                nc.sync.dma_start(out=out[b, n * P : (n + 1) * P, halves[s]], in_=terms[:, slot(s, s + 1)])
 
         w_low = [regroup_w(0, c) for c in range(PASSES)]
         for c in range(PASSES):
@@ -194,12 +207,18 @@ def tile_denseattentiononehead_pa_kernel(tc, hidden_states, W_q, cos, sin, grad_
         tokens.append(quantise_tokens(grouped[2]))
 
         for i in range(len(tiles)):
-            high_products_sum_and_store(i, gh_high if i == 0 else multiply(tokens[i], 1), terms)
+            done = terms
+            products(i, gh_high, done, 1)
+            if i + 1 == len(tiles):
+                sum_on_vector_and_store(i, done)
+                break
+            sum_on_gpsimd(done)
             if 0 < i and i + 2 < len(tiles):
                 tokens.append(quantise_tokens(grouped[i + 2]))
-            if i + 1 < len(tiles):
-                terms = low_products(i + 1, multiply(tokens[i + 1], 0))
+            terms = low_products(i + 1, multiply(tokens[i + 1], 0))
+            gh_high = multiply(tokens[i + 1], 1)
             if i + 3 < len(tiles):
                 grouped.append(turn_tokens(i + 3))
+            sum_on_tensor_and_store(i, done)
             if i % BATCH == 0 and i // BATCH + 1 < L_BLOCKS:
                 negate_sin_low(i // BATCH + 1)

@@ -21,6 +21,7 @@ PAIR = 2
 VECTOR_COLS = 352
 SLOTS = 4
 GPSIMD_COLS = 896
+LAST_CUTS = (0, 512, 896, 1024)
 RUN = 4
 
 FLOPS = 2 * BATCH * LENGTH * WIDTH * WIDTH
@@ -163,15 +164,12 @@ def tile_denseattentiononehead_pa_kernel(tc, hidden_states, W_q, cos, sin, grad_
             products(i, gh_low, terms, 0)
             return terms
 
-        def sum_on_gpsimd(terms):
+        def sum_on_gpsimd(terms, c0=0, c1=GPSIMD_COLS):
             nc.gpsimd.tensor_tensor(
-                out=terms[:, 0:GPSIMD_COLS],
-                in0=terms[:, 0:GPSIMD_COLS],
-                in1=terms[:, WIDTH : WIDTH + GPSIMD_COLS],
-                op=ADD,
+                out=terms[:, c0:c1], in0=terms[:, c0:c1], in1=terms[:, WIDTH + c0 : WIDTH + c1], op=ADD
             )
 
-        def sum_on_tensor_and_store(i, terms):
+        def sum_on_tensor_and_store(i, terms, pieces=((0, WIDTH),)):
             n, b = tiles[i]
             summed = transposed.tile([P, WIDTH - GPSIMD_COLS], F32, tag="turned")
             nc.tensor.matmul(out=summed[:], lhsT=identity[:], rhs=terms[:, GPSIMD_COLS:WIDTH], start=True, stop=False)
@@ -179,15 +177,16 @@ def tile_denseattentiononehead_pa_kernel(tc, hidden_states, W_q, cos, sin, grad_
                 out=summed[:], lhsT=identity[:], rhs=terms[:, WIDTH + GPSIMD_COLS : 2 * WIDTH], start=False, stop=True
             )
             nc.scalar.copy(out=terms[:, GPSIMD_COLS:WIDTH], in_=summed[:])
-            nc.sync.dma_start(out=out[b, n * P : (n + 1) * P, :], in_=terms[:, 0:WIDTH])
+            for c0, c1 in pieces:
+                nc.sync.dma_start(out=out[b, n * P : (n + 1) * P, c0:c1], in_=terms[:, c0:c1])
 
         def sum_on_vector_and_store(i, terms):
             n, b = tiles[i]
-            for s in range(2):
+            for c0, c1 in zip(LAST_CUTS[:-1], LAST_CUTS[1:]):
                 nc.vector.tensor_tensor(
-                    out=terms[:, slot(s, s + 1)], in0=terms[:, slot(s, s + 1)], in1=terms[:, slot(s + 2, s + 3)], op=ADD
+                    out=terms[:, c0:c1], in0=terms[:, c0:c1], in1=terms[:, WIDTH + c0 : WIDTH + c1], op=ADD
                 )
-                nc.sync.dma_start(out=out[b, n * P : (n + 1) * P, halves[s]], in_=terms[:, slot(s, s + 1)])
+                nc.sync.dma_start(out=out[b, n * P : (n + 1) * P, c0:c1], in_=terms[:, c0:c1])
 
         w_low = [regroup_w(0, c) for c in range(PASSES)]
         for c in range(PASSES):
@@ -212,13 +211,20 @@ def tile_denseattentiononehead_pa_kernel(tc, hidden_states, W_q, cos, sin, grad_
             if i + 1 == len(tiles):
                 sum_on_vector_and_store(i, done)
                 break
-            sum_on_gpsimd(done)
+            if i + 2 == len(tiles):
+                sum_on_gpsimd(done, 0, GPSIMD_COLS // 2)
+                sum_on_gpsimd(done, GPSIMD_COLS // 2, GPSIMD_COLS)
+            else:
+                sum_on_gpsimd(done)
             if 0 < i and i + 2 < len(tiles):
                 tokens.append(quantise_tokens(grouped[i + 2]))
             terms = low_products(i + 1, multiply(tokens[i + 1], 0))
             gh_high = multiply(tokens[i + 1], 1)
             if i + 3 < len(tiles):
                 grouped.append(turn_tokens(i + 3))
-            sum_on_tensor_and_store(i, done)
+            if i + 2 == len(tiles):
+                sum_on_tensor_and_store(i, done, ((0, GPSIMD_COLS // 2), (GPSIMD_COLS // 2, WIDTH)))
+            else:
+                sum_on_tensor_and_store(i, done)
             if i % BATCH == 0 and i // BATCH + 1 < L_BLOCKS:
                 negate_sin_low(i // BATCH + 1)

@@ -21,7 +21,7 @@ PAIR = 2
 VECTOR_COLS = 352
 SLOTS = 4
 GPSIMD_COLS = 896
-LAST_CUTS = (0, 512, 896, 1024)
+LAST_GPSIMD_COLS = {1: 704, 2: 768}
 RUN = 4
 
 FLOPS = 2 * BATCH * LENGTH * WIDTH * WIDTH
@@ -44,10 +44,12 @@ def tile_denseattentiononehead_pa_kernel(tc, hidden_states, W_q, cos, sin, grad_
     ):
         def load_w(h, c):
             w_tile = resident.tile([P, PACK, HALF], BF16, name="w_rows%d%d" % (h, c))
-            nc.sync.dma_start(
-                out=w_tile[:],
-                in_=W_q[c * K_PASS : (c + 1) * K_PASS, halves[h]].rearrange("(p t) j -> p t j", t=PACK),
-            )
+            for u in range(PAIR):
+                row = c * K_PASS + u * PAIR * P
+                nc.sync.dma_start(
+                    out=w_tile[:, u * PAIR : (u + 1) * PAIR, :],
+                    in_=W_q[row : row + PAIR * P, halves[h]].rearrange("(p e) j -> p e j", e=PAIR),
+                )
             return w_tile
 
         def load_tokens(n, g_tile, batches):
@@ -118,11 +120,11 @@ def tile_denseattentiononehead_pa_kernel(tc, hidden_states, W_q, cos, sin, grad_
 
         def turn_tokens(i):
             n, b = tiles[i]
-            words = g_rows[n][:].bitcast(F32).rearrange("p (b c q u) -> p b c q u", b=BATCH, c=PASSES, u=PAIR)
+            words = g_rows[n][:].bitcast(F32).rearrange("p (b c u q) -> p b c u q", b=BATCH, c=PASSES, u=PAIR)
             turned = transposed.tile([P, PASSES, PAIR, P], F32, tag="turned")
             for c in range(PASSES):
                 for u in range(PAIR):
-                    nc.tensor.transpose(turned[:, c, u, :], words[:, b, c, :, u], identity[:])
+                    nc.tensor.transpose(turned[:, c, u, :], words[:, b, c, u, :], identity[:])
             g_grouped = g_stage.tile([P, PASSES * P * PACK], BF16, align_bytes=64)
             nc.scalar.copy(
                 out=g_grouped[:].bitcast(F32).rearrange("p (c r u) -> p c r u", c=PASSES, u=PAIR),
@@ -151,11 +153,11 @@ def tile_denseattentiononehead_pa_kernel(tc, hidden_states, W_q, cos, sin, grad_
                 )
             return gh_half
 
-        def products(i, gh_half, terms, h):
+        def products(i, gh_half, terms, h, cols=slice(0, HALF)):
             nc.vector.tensor_tensor(
-                out=terms[:, slot(2 * h, 2 * h + 2)].rearrange("p (s j) -> p s j", s=2),
-                in0=gh_half[:].unsqueeze(1).to_broadcast([P, 2, HALF]),
-                in1=tables[tiles[i][0]][:, slot(2 * h, 2 * h + 2)].rearrange("p (s j) -> p s j", s=2),
+                out=terms[:, slot(2 * h, 2 * h + 2)].rearrange("p (s j) -> p s j", s=2)[:, :, cols],
+                in0=gh_half[:, cols].unsqueeze(1).to_broadcast([P, 2, cols.stop - cols.start]),
+                in1=tables[tiles[i][0]][:, slot(2 * h, 2 * h + 2)].rearrange("p (s j) -> p s j", s=2)[:, :, cols],
                 op=MULT,
             )
 
@@ -164,29 +166,23 @@ def tile_denseattentiononehead_pa_kernel(tc, hidden_states, W_q, cos, sin, grad_
             products(i, gh_low, terms, 0)
             return terms
 
-        def sum_on_gpsimd(terms, c0=0, c1=GPSIMD_COLS):
-            nc.gpsimd.tensor_tensor(
+        def add(engine, terms, c0, c1):
+            engine.tensor_tensor(
                 out=terms[:, c0:c1], in0=terms[:, c0:c1], in1=terms[:, WIDTH + c0 : WIDTH + c1], op=ADD
             )
 
-        def sum_on_tensor_and_store(i, terms, pieces=((0, WIDTH),)):
-            n, b = tiles[i]
-            summed = transposed.tile([P, WIDTH - GPSIMD_COLS], F32, tag="turned")
-            nc.tensor.matmul(out=summed[:], lhsT=identity[:], rhs=terms[:, GPSIMD_COLS:WIDTH], start=True, stop=False)
-            nc.tensor.matmul(
-                out=summed[:], lhsT=identity[:], rhs=terms[:, WIDTH + GPSIMD_COLS : 2 * WIDTH], start=False, stop=True
-            )
-            nc.scalar.copy(out=terms[:, GPSIMD_COLS:WIDTH], in_=summed[:])
-            for c0, c1 in pieces:
-                nc.sync.dma_start(out=out[b, n * P : (n + 1) * P, c0:c1], in_=terms[:, c0:c1])
+        def sum_on_tensor(terms, c0, c1):
+            summed = transposed.tile([P, c1 - c0], F32, tag="turned")
+            nc.tensor.matmul(out=summed[:], lhsT=identity[:], rhs=terms[:, c0:c1], start=True, stop=False)
+            nc.tensor.matmul(out=summed[:], lhsT=identity[:], rhs=terms[:, WIDTH + c0 : WIDTH + c1], start=False, stop=True)
+            nc.scalar.copy(out=terms[:, c0:c1], in_=summed[:])
 
-        def sum_on_vector_and_store(i, terms):
+        def store(i, terms, c0, c1):
             n, b = tiles[i]
-            for c0, c1 in zip(LAST_CUTS[:-1], LAST_CUTS[1:]):
-                nc.vector.tensor_tensor(
-                    out=terms[:, c0:c1], in0=terms[:, c0:c1], in1=terms[:, WIDTH + c0 : WIDTH + c1], op=ADD
-                )
-                nc.sync.dma_start(out=out[b, n * P : (n + 1) * P, c0:c1], in_=terms[:, c0:c1])
+            nc.sync.dma_start(out=out[b, n * P : (n + 1) * P, c0:c1], in_=terms[:, c0:c1])
+
+        def gpsimd_cols(i):
+            return LAST_GPSIMD_COLS.get(len(tiles) - 1 - i, GPSIMD_COLS)
 
         w_low = [regroup_w(0, c) for c in range(PASSES)]
         for c in range(PASSES):
@@ -205,26 +201,42 @@ def tile_denseattentiononehead_pa_kernel(tc, hidden_states, W_q, cos, sin, grad_
         gh_high = multiply(tokens[0], 1)
         tokens.append(quantise_tokens(grouped[2]))
 
-        for i in range(len(tiles)):
+        last = len(tiles) - 1
+        for i in range(last):
             done = terms
             products(i, gh_high, done, 1)
-            if i + 1 == len(tiles):
-                sum_on_vector_and_store(i, done)
-                break
-            if i + 2 == len(tiles):
-                sum_on_gpsimd(done, 0, GPSIMD_COLS // 2)
-                sum_on_gpsimd(done, GPSIMD_COLS // 2, GPSIMD_COLS)
+            g_cols = gpsimd_cols(i)
+            if i + 1 == last:
+                add(nc.gpsimd, done, 0, g_cols // 2)
+                add(nc.gpsimd, done, g_cols // 2, g_cols)
             else:
-                sum_on_gpsimd(done)
-            if 0 < i and i + 2 < len(tiles):
+                add(nc.gpsimd, done, 0, g_cols)
+            if 0 < i and i + 2 <= last:
                 tokens.append(quantise_tokens(grouped[i + 2]))
-            terms = low_products(i + 1, multiply(tokens[i + 1], 0))
+            gh_low = multiply(tokens[i + 1], 0)
+            if i + 1 < last:
+                terms = low_products(i + 1, gh_low)
             gh_high = multiply(tokens[i + 1], 1)
-            if i + 3 < len(tiles):
+            if i + 3 <= last:
                 grouped.append(turn_tokens(i + 3))
-            if i + 2 == len(tiles):
-                sum_on_tensor_and_store(i, done, ((0, GPSIMD_COLS // 2), (GPSIMD_COLS // 2, WIDTH)))
+            sum_on_tensor(done, g_cols, WIDTH)
+            if i + 1 == last:
+                store(i, done, 0, g_cols // 2)
+                store(i, done, g_cols // 2, WIDTH)
             else:
-                sum_on_tensor_and_store(i, done)
+                store(i, done, 0, WIDTH)
             if i % BATCH == 0 and i // BATCH + 1 < L_BLOCKS:
                 negate_sin_low(i // BATCH + 1)
+
+        terms = results.tile([P, SLOTS * HALF], F32)
+        for cols in (slice(0, HALF // 2), slice(HALF // 2, HALF)):
+            products(last, gh_low, terms, 0, cols)
+            products(last, gh_high, terms, 1, cols)
+        add(nc.gpsimd, terms, 0, HALF // 2)
+        store(last, terms, 0, HALF // 2)
+        sum_on_tensor(terms, HALF, HALF + HALF // 2)
+        store(last, terms, HALF, HALF + HALF // 2)
+        add(nc.vector, terms, HALF // 2, HALF)
+        store(last, terms, HALF // 2, HALF)
+        add(nc.vector, terms, HALF + HALF // 2, WIDTH)
+        store(last, terms, HALF + HALF // 2, WIDTH)

@@ -20,7 +20,7 @@ L_BLOCKS = LENGTH // P
 PAIR = 2
 VECTOR_COLS = 352
 SLOTS = 4
-GPSIMD_COLS = 896
+GPSIMD_COLS = 832
 LAST_GPSIMD_COLS = {1: 704, 2: 768}
 RUN = 4
 
@@ -98,6 +98,9 @@ def tile_denseattentiononehead_pa_kernel(tc, hidden_states, W_q, cos, sin, grad_
 
         identity = resident.tile([P, P], F32, name="identity")
         make_identity(nc, identity[:])
+        first_copy = resident.tile([P, PAIR], F32, name="first_copy")
+        nc.gpsimd.memset(first_copy[:], 0.0)
+        nc.scalar.copy(out=first_copy[:, 1:2], in_=first_copy[:, 0:1])
 
         w_codes = resident.tile([P, PASSES, WIDTH], U32, name="w_codes", align_bytes=64)
         w_scales = resident.tile([P, PASSES, WIDTH], U8, name="w_scales", align_bytes=64)

import concourse.mybir as mybir
from concourse.masks import make_identity

F32 = mybir.dt.float32
BF16 = mybir.dt.bfloat16
U32 = mybir.dt.uint32
U8 = mybir.dt.uint8
E4M3_X4 = mybir.dt.float8_e4m3fn_x4
E5M2_X4 = mybir.dt.float8_e5m2_x4
MULT = mybir.AluOpType.mult
ADD = mybir.AluOpType.add

BATCH, LENGTH, WIDTH = 2, 1024, 1024
HALF = WIDTH // 2
P = 128
PACK = 4
K_PASS = P * PACK
PASSES = WIDTH // K_PASS
L_BLOCKS = LENGTH // P
PAIR = 2
VECTOR_COLS = 352
SLOTS = 4
GPSIMD_COLS = 832
LAST_GPSIMD_COLS = {1: 704, 2: 768}
RUN = 4

FLOPS = 2 * BATCH * LENGTH * WIDTH * WIDTH
BYTES = 2 * (BATCH * LENGTH * WIDTH + 3 * WIDTH * WIDTH) + 4 * BATCH * LENGTH * WIDTH


def tile_denseattentiononehead_pa_kernel(tc, hidden_states, W_q, cos, sin, grad_out, out):
    nc = tc.nc
    low, high = slice(0, HALF), slice(HALF, WIDTH)
    halves = (low, high)
    tiles = [(n, b) for n in range(L_BLOCKS) for b in range(BATCH)]
    with (
        tc.tile_pool(name="resident", bufs=1) as resident,
        tc.tile_pool(name="w_stage", bufs=PASSES * 2) as w_stage,
        tc.tile_pool(name="g_stage", bufs=4) as g_stage,
        tc.tile_pool(name="results", bufs=8) as results,
        tc.psum_pool(name="transposed", bufs=2) as transposed,
        tc.psum_pool(name="gh", bufs=3) as gh_pool,
        tc.manual_schedule(),
    ):
        def load_w(h, c):
            w_tile = resident.tile([P, PACK, HALF], BF16, name="w_rows%d%d" % (h, c))
            for u in range(PAIR):
                row = c * K_PASS + u * PAIR * P
                nc.sync.dma_start(
                    out=w_tile[:, u * PAIR : (u + 1) * PAIR, :],
                    in_=W_q[row : row + PAIR * P, halves[h]].rearrange("(p e) j -> p e j", e=PAIR),
                )
            return w_tile

        def load_tokens(n, g_tile, batches):
            b0, b1 = batches[0], batches[-1] + 1
            nc.sync.dma_start(
                out=g_tile[:, b0 * WIDTH : b1 * WIDTH].rearrange("p (b o) -> p b o", b=b1 - b0),
                in_=grad_out[b0:b1, n * P : (n + 1) * P, :].rearrange("b p o -> p b o"),
            )

        def slot(s0, s1):
            return slice(s0 * HALF, s1 * HALF)

        def load_slot(table, n, s, half):
            nc.sync.dma_start(out=tables[n][:, slot(s, s + 1)], in_=table[n * P : (n + 1) * P, half])

        def load_tables(n):
            positions = slice(n * P, (n + 1) * P)
            nc.sync.dma_start(
                out=tables[n][:].rearrange("p (s j) -> p s j", s=SLOTS)[:, 0 : SLOTS : SLOTS - 1, :],
                in_=cos[positions, :].rearrange("p (h j) -> p h j", h=2),
            )
            nc.sync.dma_start(out=tables[n][:, slot(1, 3)], in_=sin[positions, :])

        def negate_sin_low(n):
            nc.scalar.mul(out=tables[n][:, slot(1, 2)], in_=tables[n][:, slot(1, 2)], mul=-1.0)

        g_rows = [resident.tile([P, BATCH * WIDTH], BF16, name="g_rows%d" % n) for n in range(L_BLOCKS)]
        tables = [resident.tile([P, SLOTS * HALF], BF16, name="tables%d" % n) for n in range(L_BLOCKS)]
        w_rows = {}
        for c in range(PASSES):
            w_rows[(0, c)] = load_w(0, c)
        load_tokens(0, g_rows[0], (0,))
        for c in range(PASSES):
            w_rows[(1, c)] = load_w(1, c)
        load_slot(sin, 0, 1, low)
        load_slot(cos, 0, 0, low)
        load_tokens(0, g_rows[0], (1,))
        load_tokens(1, g_rows[1], (0,))
        load_slot(sin, 0, 2, high)
        load_slot(cos, 0, 3, high)
        load_tokens(1, g_rows[1], (1,))
        for n in range(1, L_BLOCKS):
            if n + 1 < L_BLOCKS:
                load_tokens(n + 1, g_rows[n + 1], (0, 1))
            load_tables(n)

        identity = resident.tile([P, P], F32, name="identity")
        make_identity(nc, identity[:])
        first_copy = resident.tile([P, PAIR], F32, name="first_copy")
        nc.gpsimd.memset(first_copy[:], 0.0)
        nc.scalar.copy(out=first_copy[:, 1:2], in_=first_copy[:, 0:1])

        w_codes = resident.tile([P, PASSES, WIDTH], U32, name="w_codes", align_bytes=64)
        w_scales = resident.tile([P, PASSES, WIDTH], U8, name="w_scales", align_bytes=64)

        def regroup_w(h, c):
            w_grouped = w_stage.tile([P, HALF * PACK], BF16, align_bytes=64)
            for copy, cols in ((nc.vector.tensor_copy, slice(0, VECTOR_COLS)), (nc.scalar.copy, slice(VECTOR_COLS, HALF))):
                copy(
                    out=w_grouped[:, cols.start * PACK : cols.stop * PACK].rearrange("p (m i t) -> p m t i", i=RUN, t=PACK),
                    in_=w_rows[(h, c)][:, :, cols].rearrange("p t (m i) -> p m t i", i=RUN),
                )
            return w_grouped

        def quantise_w(h, c, w_grouped):
            nc.vector.quantize_mx(
                out=w_codes[:, c, halves[h]].bitcast(E4M3_X4),
                scales=w_scales[:, c, halves[h]],
                in_=w_grouped[:],
            )

        def turn_tokens(i):
            n, b = tiles[i]
            words = g_rows[n][:].bitcast(F32).rearrange("p (b c u q) -> p b c u q", b=BATCH, c=PASSES, u=PAIR)
            turned = transposed.tile([P, PASSES, PAIR, P], F32, tag="turned")
            for c in range(PASSES):
                for u in range(PAIR):
                    nc.tensor.transpose(turned[:, c, u, :], words[:, b, c, u, :], identity[:])
            g_grouped = g_stage.tile([P, PASSES * P * PACK], BF16, align_bytes=64)
            nc.scalar.copy(
                out=g_grouped[:].bitcast(F32).rearrange("p (c r u) -> p c r u", c=PASSES, u=PAIR),
                in_=turned[:].rearrange("p c u r -> p c r u"),
            )
            return g_grouped

        def quantise_tokens(g_grouped):
            g_codes = g_stage.tile([P, PASSES * P], U32, align_bytes=64)
            g_scales = g_stage.tile([P, PASSES * P], U8, align_bytes=64)
            nc.vector.quantize_mx(out=g_codes[:].bitcast(E5M2_X4), scales=g_scales[:], in_=g_grouped[:])
            return g_codes, g_scales

        def multiply(tile_tokens, h):
            g_codes, g_scales = tile_tokens
            gh_half = gh_pool.tile([P, HALF], F32, tag="gh_half%d" % h)
            for c in range(PASSES):
                nc.tensor.matmul_mx(
                    out=gh_half[:],
                    lhsT=g_codes[:, c * P : (c + 1) * P].bitcast(E5M2_X4),
                    lhsT_scale=g_scales[:, c * P : (c + 1) * P],
                    rhs=w_codes[:, c, halves[h]].bitcast(E4M3_X4),
                    rhs_scale=w_scales[:, c, halves[h]],
                    start=(c == 0),
                    stop=(c == PASSES - 1),
                )
            return gh_half

        def products(i, gh_half, terms, h, cols=slice(0, HALF)):
            nc.vector.tensor_tensor(
                out=terms[:, slot(2 * h, 2 * h + 2)].rearrange("p (s j) -> p s j", s=2)[:, :, cols],
                in0=gh_half[:, cols].unsqueeze(1).to_broadcast([P, 2, cols.stop - cols.start]),
                in1=tables[tiles[i][0]][:, slot(2 * h, 2 * h + 2)].rearrange("p (s j) -> p s j", s=2)[:, :, cols],
                op=MULT,
            )

        def low_products(i, gh_low):
            terms = results.tile([P, SLOTS * HALF], F32)
            products(i, gh_low, terms, 0)
            return terms

        def add(engine, terms, c0, c1):
            engine.tensor_tensor(
                out=terms[:, c0:c1], in0=terms[:, c0:c1], in1=terms[:, WIDTH + c0 : WIDTH + c1], op=ADD
            )

        def sum_on_tensor(terms, c0, c1):
            summed = transposed.tile([P, c1 - c0], F32, tag="turned")
            nc.tensor.matmul(out=summed[:], lhsT=identity[:], rhs=terms[:, c0:c1], start=True, stop=False)
            nc.tensor.matmul(out=summed[:], lhsT=identity[:], rhs=terms[:, WIDTH + c0 : WIDTH + c1], start=False, stop=True)
            nc.scalar.copy(out=terms[:, c0:c1], in_=summed[:])

        def store(i, terms, c0, c1):
            n, b = tiles[i]
            nc.sync.dma_start(out=out[b, n * P : (n + 1) * P, c0:c1], in_=terms[:, c0:c1])

        def gpsimd_cols(i):
            return LAST_GPSIMD_COLS.get(len(tiles) - 1 - i, GPSIMD_COLS)

        w_low = [regroup_w(0, c) for c in range(PASSES)]
        for c in range(PASSES):
            quantise_w(0, c, w_low[c])
        grouped = [turn_tokens(0)]
        w_high = [regroup_w(1, 0)]
        tokens = [quantise_tokens(grouped[0])]
        w_high.append(regroup_w(1, 1))
        negate_sin_low(0)
        for c in range(PASSES):
            quantise_w(1, c, w_high[c])
        terms = low_products(0, multiply(tokens[0], 0))
        grouped.append(turn_tokens(1))
        grouped.append(turn_tokens(2))
        tokens.append(quantise_tokens(grouped[1]))
        gh_high = multiply(tokens[0], 1)
        tokens.append(quantise_tokens(grouped[2]))

        last = len(tiles) - 1
        for i in range(last):
            done = terms
            products(i, gh_high, done, 1)
            g_cols = gpsimd_cols(i)
            if i + 1 == last:
                add(nc.gpsimd, done, 0, g_cols // 2)
                add(nc.gpsimd, done, g_cols // 2, g_cols)
            else:
                add(nc.gpsimd, done, 0, g_cols)
            if 0 < i and i + 2 <= last:
                tokens.append(quantise_tokens(grouped[i + 2]))
            gh_low = multiply(tokens[i + 1], 0)
            if i + 1 < last:
                terms = low_products(i + 1, gh_low)
            gh_high = multiply(tokens[i + 1], 1)
            if i + 3 <= last:
                grouped.append(turn_tokens(i + 3))
            sum_on_tensor(done, g_cols, WIDTH)
            if i + 1 == last:
                store(i, done, 0, g_cols // 2)
                store(i, done, g_cols // 2, WIDTH)
            else:
                store(i, done, 0, WIDTH)
            if i % BATCH == 0 and i // BATCH + 1 < L_BLOCKS:
                negate_sin_low(i // BATCH + 1)

        terms = results.tile([P, SLOTS * HALF], F32)
        for cols in (slice(0, HALF // 2), slice(HALF // 2, HALF)):
            products(last, gh_low, terms, 0, cols)
            products(last, gh_high, terms, 1, cols)
        add(nc.gpsimd, terms, 0, HALF // 2)
        store(last, terms, 0, HALF // 2)
        sum_on_tensor(terms, HALF, HALF + HALF // 2)
        store(last, terms, HALF, HALF + HALF // 2)
        add(nc.vector, terms, HALF // 2, HALF)
        store(last, terms, HALF // 2, HALF)
        add(nc.vector, terms, HALF + HALF // 2, WIDTH)
        store(last, terms, HALF + HALF // 2, WIDTH)
